import numpy as np
import ml_dtypes


def mxq(x, axis, fmt="e4m3"):
    dtype, down = {"e4m3": (ml_dtypes.float8_e4m3fn, 7), "e5m2": (ml_dtypes.float8_e5m2, 14)}[fmt]
    v = np.moveaxis(np.asarray(x, np.float32).astype(ml_dtypes.bfloat16).astype(np.float64), axis, -1)
    blocks = v.reshape(v.shape[:-1] + (-1, 32))
    amax = np.abs(blocks).max(-1, keepdims=True)
    byte = np.maximum(np.where(amax > 0, np.frexp(amax)[1] - 1 + 127, 0) - down, 1)
    scale = np.exp2(byte - 127.0)
    codes = (blocks / scale).astype(np.float32).astype(dtype).astype(np.float64)
    return np.moveaxis((codes * scale).reshape(v.shape), -1, axis)


WIDE = False


def mx_kscale(k):
    if not WIDE:
        return np.ones(k)
    levels = np.array([10, -10, 5, -5, 0])
    a = np.random.permutation(np.resize(levels, k // 512 * 4)).reshape(k // 512, 4)
    idx = np.arange(k)
    return np.exp2(a[idx // 512, idx % 128 // 32])


BF16 = ml_dtypes.bfloat16


def bf(x):
    return np.asarray(x, np.float32).astype(BF16)


def f64(x):
    return np.asarray(x).astype(np.float64)


B, N, D, F1, F2, F3, G1, G2 = 4, 64, 512, 1024, 128, 512, 512, 512
ALPHA = 0.2


def lrelu(v):
    return np.maximum(v, ALPHA * v)


def setup_inputs():
    s, t = mx_kscale(D), mx_kscale(F1)
    ss = np.concatenate([s, s])
    return {"x": bf(np.random.standard_normal((B, N, D)) * s),
            "fe_w0": bf(np.random.standard_normal((D + D, F1)) / np.sqrt(D + D) / ss[:, None] * t),
            "fe_b0": bf(np.random.standard_normal(F1) * 0.3 * t),
            "fe_w1": bf(np.random.standard_normal((F1, F2)) * 1.4 / np.sqrt(F1) / t[:, None]),
            "fe_b1": bf(np.random.standard_normal(F2) * 0.3)}


def reference(x, fe_w0, fe_b0, fe_w1, fe_b1):
    xq = mxq(f64(x), 2, "e4m3")
    w0 = f64(fe_w0)
    u = xq @ mxq(w0[:D], 0, "e4m3")
    v = xq @ mxq(w0[D:], 0, "e4m3")
    e1 = lrelu(u[:, :, None, :] + v[:, None, :, :] + f64(fe_b0))
    return lrelu((mxq(e1, 3, "e4m3") @ mxq(f64(fe_w1), 0, "e4m3")) + f64(fe_b1))

@@ -1,0 +1,224 @@
+from contextlib import ExitStack
+
+import concourse.mybir as mybir
+from concourse.masks import make_identity
+
+BF16 = mybir.dt.bfloat16
+F32 = mybir.dt.float32
+U32 = mybir.dt.uint32
+U8 = mybir.dt.uint8
+FP8X4 = mybir.dt.float8_e4m3fn_x4
+ADD = mybir.AluOpType.add
+MULT = mybir.AluOpType.mult
+MAX = mybir.AluOpType.max
+IDENTITY = mybir.ActivationFunctionType.Identity
+
+P = 128
+PACK = 4
+K_PASS = P * PACK
+
+GRAPHS, NODES, D_IN, HIDDEN, D_OUT = 4, 64, 512, 1024, 128
+ROWS = GRAPHS * NODES
+ROW_TILES = ROWS // P
+HALVES = 2
+PASSES = HIDDEN // K_PASS
+FEATURE_TILES = HIDDEN // P
+ALPHA = 0.2
+
+I_PER_BLOCK = 8
+PAIRS = I_PER_BLOCK * NODES
+PAIR_TILES = PAIRS // P
+BLOCKS = ROWS // I_PER_BLOCK
+BLOCKS_PER_GRAPH = NODES // I_PER_BLOCK
+
+FLOPS = 2 * HALVES * ROWS * D_IN * HIDDEN + 2 * ROWS * NODES * HIDDEN * D_OUT
+
+
+def side_by_side(copy, grouped, planes):
+    copy(
+        out=grouped.rearrange("p (g i) t -> p g t i", i=4),
+        in_=planes.rearrange("p t (g i) -> p g t i", i=4),
+    )
+
+
+def tile_graph_gan_pa_t_kernel(tc, x, fe_w0, fe_b0, fe_w1, fe_b1, out):
+    nc = tc.nc
+    x_rows = x.flatten_outer_dims()
+    out_rows = out.flatten_outer_dims()
+
+    with ExitStack() as stack:
+        keep = stack.enter_context(tc.tile_pool(name="keep", bufs=1))
+        sums = stack.enter_context(tc.tile_pool(name="sums", bufs=3))
+        hidden = stack.enter_context(tc.tile_pool(name="hidden", bufs=3))
+        results = stack.enter_context(tc.tile_pool(name="results", bufs=3))
+        psum_head = stack.enter_context(tc.psum_pool(name="psum_head", bufs=2))
+        psum_out = stack.enter_context(tc.psum_pool(name="psum_out", bufs=4))
+
+        identity = keep.tile([P, P], BF16)
+        make_identity(nc, identity[:])
+        b0_rows = keep.tile([P, P], BF16)
+        nc.gpsimd.memset(b0_rows[:], 0.0)
+
+        x_sb = keep.tile([P, ROW_TILES, D_IN], BF16)
+        nc.sync.dma_start(out=x_sb[:], in_=x_rows.rearrange("(r p) d -> p r d", p=P))
+        nc.scalar.dma_start(
+            out=b0_rows[0:FEATURE_TILES, :], in_=fe_b0.rearrange("(r p) -> r p", p=P)
+        )
+        w0_planes = keep.tile([P, HALVES, PACK, HIDDEN], BF16)
+        for c in range(PASSES):
+            f_cols = slice(c * K_PASS, (c + 1) * K_PASS)
+            for h in range(HALVES):
+                nc.sync.dma_start(
+                    out=w0_planes[:, h, :, f_cols],
+                    in_=fe_w0[h * D_IN : (h + 1) * D_IN, f_cols].rearrange(
+                        "(t p) f -> p t f", p=P
+                    ),
+                )
+        w1_planes = keep.tile([P, PASSES, PACK, D_OUT], BF16)
+        nc.sync.dma_start(
+            out=w1_planes[:], in_=fe_w1.rearrange("(c t p) n -> p c t n", t=PACK, p=P)
+        )
+        b1_bf16 = keep.tile([P, D_OUT], BF16)
+        nc.sync.dma_start(out=b1_bf16[:], in_=fe_b1.partition_broadcast(P))
+
+        x_grouped = keep.tile([P, ROWS, PACK], BF16, align_bytes=64)
+        for r in range(ROW_TILES):
+            x_t = psum_head.tile([P, PACK, P], BF16, tag="transposed")
+            for t in range(PACK):
+                nc.tensor.transpose(x_t[:, t, :], x_sb[:, r, t * P : (t + 1) * P], identity[:])
+            nc.vector.tensor_copy(
+                out=x_grouped[:, r * P : (r + 1) * P, :], in_=x_t[:].rearrange("p t r -> p r t")
+            )
+        x_codes = keep.tile([P, ROWS], U32, align_bytes=64)
+        x_scales = keep.tile([P, ROWS], U8, align_bytes=64)
+        nc.vector.quantize_mx(
+            out=x_codes[:].bitcast(FP8X4),
+            scales=x_scales[:],
+            in_=x_grouped[:].rearrange("p r t -> p (r t)"),
+        )
+
+        b0_t = psum_head.tile([P, P], BF16, tag="transposed")
+        nc.tensor.transpose(b0_t[:], b0_rows[:], identity[:])
+        b0 = keep.tile([P, FEATURE_TILES], F32)
+        nc.vector.tensor_copy(out=b0[:], in_=b0_t[:, 0:FEATURE_TILES])
+
+        w0_grouped = keep.tile([P, HALVES, HIDDEN, PACK], BF16, align_bytes=64)
+        w0_codes = keep.tile([P, HALVES, HIDDEN], U32, align_bytes=64)
+        w0_scales = keep.tile([P, HALVES, HIDDEN], U8, align_bytes=64)
+        u_b0 = keep.tile([P, FEATURE_TILES, ROWS], F32)
+        v = keep.tile([P, FEATURE_TILES, ROWS], F32)
+        for c in range(PASSES):
+            f_cols = slice(c * K_PASS, (c + 1) * K_PASS)
+            for h in range(HALVES):
+                side_by_side(
+                    nc.vector.tensor_copy, w0_grouped[:, h, f_cols, :], w0_planes[:, h, :, f_cols]
+                )
+            for h in range(HALVES):
+                nc.vector.quantize_mx(
+                    out=w0_codes[:, h, f_cols].bitcast(FP8X4),
+                    scales=w0_scales[:, h, f_cols],
+                    in_=w0_grouped[:, h, f_cols, :].rearrange("p f t -> p (f t)"),
+                )
+            for ft in range(c * PACK, (c + 1) * PACK):
+                tile_cols = slice(ft * P, (ft + 1) * P)
+                uv = psum_head.tile([P, HALVES, ROWS], F32)
+                for h in range(HALVES):
+                    nc.tensor.matmul_mx(
+                        out=uv[:, h, :],
+                        lhsT=w0_codes[:, h, tile_cols].bitcast(FP8X4),
+                        lhsT_scale=w0_scales[:, h, tile_cols],
+                        rhs=x_codes[:].bitcast(FP8X4),
+                        rhs_scale=x_scales[:],
+                        start=True,
+                        stop=True,
+                    )
+                nc.scalar.activation(
+                    out=u_b0[:, ft, :], in_=uv[:, 0, :], func=IDENTITY, bias=b0[:, ft : ft + 1], scale=1.0
+                )
+                nc.vector.tensor_copy(out=v[:, ft, :], in_=uv[:, 1, :])
+
+        w1_grouped = keep.tile([P, PASSES, D_OUT, PACK], BF16, align_bytes=64)
+        for c in range(PASSES):
+            side_by_side(nc.scalar.copy, w1_grouped[:, c, :, :], w1_planes[:, c, :, :])
+        w1_codes = keep.tile([P, PASSES, D_OUT], U32, align_bytes=64)
+        w1_scales = keep.tile([P, PASSES, D_OUT], U8, align_bytes=64)
+        nc.vector.quantize_mx(
+            out=w1_codes[:].rearrange("p c n -> p (c n)").bitcast(FP8X4),
+            scales=w1_scales[:].rearrange("p c n -> p (c n)"),
+            in_=w1_grouped[:].rearrange("p c n t -> p (c n t)"),
+        )
+        b1 = keep.tile([P, D_OUT], F32)
+        nc.vector.tensor_copy(out=b1[:], in_=b1_bf16[:])
+
+        def hidden_layer(block):
+            j_rows = slice((block // BLOCKS_PER_GRAPH) * NODES, (block // BLOCKS_PER_GRAPH + 1) * NODES)
+            z = sums.tile([P, PASSES, PACK, PAIRS], F32)
+            for c in range(PASSES):
+                for t in range(PACK):
+                    ft = c * PACK + t
+                    for i in range(I_PER_BLOCK):
+                        i_row = block * I_PER_BLOCK + i
+                        nc.scalar.activation(
+                            out=z[:, c, t, i * NODES : (i + 1) * NODES],
+                            in_=v[:, ft, j_rows],
+                            func=IDENTITY,
+                            bias=u_b0[:, ft, i_row : i_row + 1],
+                            scale=1.0,
+                        )
+            e1 = hidden.tile([P, PASSES, PAIRS, PACK], BF16, align_bytes=64)
+            for c in range(PASSES):
+                z_words = z[:, c, :, :].rearrange("p t w -> p w t")
+                nc.vector.scalar_tensor_tensor(
+                    out=e1[:, c, :, :], in0=z_words, scalar=ALPHA, in1=z_words, op0=MULT, op1=MAX
+                )
+            codes = hidden.tile([P, PASSES, PAIRS], U32, align_bytes=64)
+            scales = hidden.tile([P, PASSES, PAIRS], U8, align_bytes=64)
+            for c in range(PASSES):
+                nc.vector.quantize_mx(
+                    out=codes[:, c, :].bitcast(FP8X4),
+                    scales=scales[:, c, :],
+                    in_=e1[:, c, :, :].rearrange("p w t -> p (w t)"),
+                )
+            return codes, scales
+
+        def second_product(codes, scales):
+            y = psum_out.tile([P, PAIR_TILES, D_OUT], F32)
+            for g in range(PAIR_TILES):
+                pair_cols = slice(g * P, (g + 1) * P)
+                for c in range(PASSES):
+                    nc.tensor.matmul_mx(
+                        out=y[:, g, :],
+                        lhsT=codes[:, c, pair_cols].bitcast(FP8X4),
+                        lhsT_scale=scales[:, c, pair_cols],
+                        rhs=w1_codes[:, c, :].bitcast(FP8X4),
+                        rhs_scale=w1_scales[:, c, :],
+                        start=(c == 0),
+                        stop=(c == PASSES - 1),
+                    )
+            return y
+
+        def finish(block, y):
+            biased = results.tile([P, PAIR_TILES, D_OUT], F32)
+            nc.vector.tensor_tensor(
+                out=biased[:],
+                in0=y[:],
+                in1=b1[:].unsqueeze(1).to_broadcast([P, PAIR_TILES, D_OUT]),
+                op=ADD,
+            )
+            result = results.tile([P, PAIR_TILES, D_OUT], F32)
+            nc.vector.scalar_tensor_tensor(
+                out=result[:], in0=biased[:], scalar=ALPHA, in1=biased[:], op0=MULT, op1=MAX
+            )
+            nc.sync.dma_start(
+                out=out_rows[block * PAIRS : (block + 1) * PAIRS, :].rearrange("(g p) n -> p g n", p=P),
+                in_=result[:],
+            )
+
+        waiting = None
+        for block in range(BLOCKS):
+            codes, scales = hidden_layer(block)
+            y = second_product(codes, scales)
+            if waiting is not None:
+                finish(block - 1, waiting)
+            waiting = y
+        finish(BLOCKS - 1, waiting)

@@ -30,6 +30,9 @@ PAIRS = I_PER_BLOCK * NODES
 PAIR_TILES = PAIRS // P
 BLOCKS = ROWS // I_PER_BLOCK
 BLOCKS_PER_GRAPH = NODES // I_PER_BLOCK
+I_VIA_SCALAR = 2
+PAIRS_DIRECT = (I_PER_BLOCK - I_VIA_SCALAR) * NODES
+PAIRS_VIA_SCALAR = I_VIA_SCALAR * NODES
 
 FLOPS = 2 * HALVES * ROWS * D_IN * HIDDEN + 2 * ROWS * NODES * HIDDEN * D_OUT
 
@@ -166,11 +169,17 @@ def tile_graph_gan_pa_t_kernel(tc, x, fe_w0, fe_b0, fe_w1, fe_b1, out):
                             scale=1.0,
                         )
             e1 = hidden.tile([P, PASSES, PAIRS, PACK], BF16, align_bytes=64)
+            e1_planes = hidden.tile([P, PASSES, PACK, PAIRS_VIA_SCALAR], BF16)
             for c in range(PASSES):
-                z_words = z[:, c, :, :].rearrange("p t w -> p w t")
+                z_words = z[:, c, :, 0:PAIRS_DIRECT].rearrange("p t w -> p w t")
                 nc.vector.scalar_tensor_tensor(
-                    out=e1[:, c, :, :], in0=z_words, scalar=ALPHA, in1=z_words, op0=MULT, op1=MAX
+                    out=e1[:, c, 0:PAIRS_DIRECT, :], in0=z_words, scalar=ALPHA, in1=z_words, op0=MULT, op1=MAX
                 )
+                z_planes = z[:, c, :, PAIRS_DIRECT:PAIRS]
+                nc.vector.scalar_tensor_tensor(
+                    out=e1_planes[:, c, :, :], in0=z_planes, scalar=ALPHA, in1=z_planes, op0=MULT, op1=MAX
+                )
+                side_by_side(nc.scalar.copy, e1[:, c, PAIRS_DIRECT:PAIRS, :], e1_planes[:, c, :, :])
             codes = hidden.tile([P, PASSES, PAIRS], U32, align_bytes=64)
             scales = hidden.tile([P, PASSES, PAIRS], U8, align_bytes=64)
             for c in range(PASSES):

@@ -30,9 +30,7 @@ PAIRS = I_PER_BLOCK * NODES
 PAIR_TILES = PAIRS // P
 BLOCKS = ROWS // I_PER_BLOCK
 BLOCKS_PER_GRAPH = NODES // I_PER_BLOCK
-I_VIA_SCALAR = 2
-PAIRS_DIRECT = (I_PER_BLOCK - I_VIA_SCALAR) * NODES
-PAIRS_VIA_SCALAR = I_VIA_SCALAR * NODES
+SUMS_AHEAD = 2
 
 FLOPS = 2 * HALVES * ROWS * D_IN * HIDDEN + 2 * ROWS * NODES * HIDDEN * D_OUT
 
@@ -51,21 +49,26 @@ def tile_graph_gan_pa_t_kernel(tc, x, fe_w0, fe_b0, fe_w1, fe_b1, out):
 
     with ExitStack() as stack:
         keep = stack.enter_context(tc.tile_pool(name="keep", bufs=1))
-        sums = stack.enter_context(tc.tile_pool(name="sums", bufs=3))
+        sums = stack.enter_context(tc.tile_pool(name="sums", bufs=SUMS_AHEAD + 1))
         hidden = stack.enter_context(tc.tile_pool(name="hidden", bufs=3))
         results = stack.enter_context(tc.tile_pool(name="results", bufs=3))
         psum_head = stack.enter_context(tc.psum_pool(name="psum_head", bufs=2))
-        psum_out = stack.enter_context(tc.psum_pool(name="psum_out", bufs=4))
+        psum_out = stack.enter_context(tc.psum_pool(name="psum_out", bufs=2))
 
-        identity = keep.tile([P, P], BF16)
-        make_identity(nc, identity[:])
-        b0_rows = keep.tile([P, P], BF16)
-        nc.gpsimd.memset(b0_rows[:], 0.0)
+        identity_bf16 = keep.tile([P, P], BF16)
+        make_identity(nc, identity_bf16[:])
+        identity_f32 = keep.tile([P, P], F32)
+        make_identity(nc, identity_f32[:])
+        bias_rows = keep.tile([P, P], BF16)
+        nc.gpsimd.memset(bias_rows[:], 0.0)
 
         x_sb = keep.tile([P, ROW_TILES, D_IN], BF16)
         nc.sync.dma_start(out=x_sb[:], in_=x_rows.rearrange("(r p) d -> p r d", p=P))
         nc.scalar.dma_start(
-            out=b0_rows[0:FEATURE_TILES, :], in_=fe_b0.rearrange("(r p) -> r p", p=P)
+            out=bias_rows[0:FEATURE_TILES, :], in_=fe_b0.rearrange("(r p) -> r p", p=P)
+        )
+        nc.scalar.dma_start(
+            out=bias_rows[FEATURE_TILES : FEATURE_TILES + 1, :], in_=fe_b1.rearrange("(r p) -> r p", p=P)
         )
         w0_planes = keep.tile([P, HALVES, PACK, HIDDEN], BF16)
         for c in range(PASSES):
@@ -81,14 +84,12 @@ def tile_graph_gan_pa_t_kernel(tc, x, fe_w0, fe_b0, fe_w1, fe_b1, out):
         nc.sync.dma_start(
             out=w1_planes[:], in_=fe_w1.rearrange("(c t p) n -> p c t n", t=PACK, p=P)
         )
-        b1_bf16 = keep.tile([P, D_OUT], BF16)
-        nc.sync.dma_start(out=b1_bf16[:], in_=fe_b1.partition_broadcast(P))
 
         x_grouped = keep.tile([P, ROWS, PACK], BF16, align_bytes=64)
         for r in range(ROW_TILES):
             x_t = psum_head.tile([P, PACK, P], BF16, tag="transposed")
             for t in range(PACK):
-                nc.tensor.transpose(x_t[:, t, :], x_sb[:, r, t * P : (t + 1) * P], identity[:])
+                nc.tensor.transpose(x_t[:, t, :], x_sb[:, r, t * P : (t + 1) * P], identity_bf16[:])
             nc.vector.tensor_copy(
                 out=x_grouped[:, r * P : (r + 1) * P, :], in_=x_t[:].rearrange("p t r -> p r t")
             )
@@ -100,10 +101,13 @@ def tile_graph_gan_pa_t_kernel(tc, x, fe_w0, fe_b0, fe_w1, fe_b1, out):
             in_=x_grouped[:].rearrange("p r t -> p (r t)"),
         )
 
-        b0_t = psum_head.tile([P, P], BF16, tag="transposed")
-        nc.tensor.transpose(b0_t[:], b0_rows[:], identity[:])
-        b0 = keep.tile([P, FEATURE_TILES], F32)
-        nc.vector.tensor_copy(out=b0[:], in_=b0_t[:, 0:FEATURE_TILES])
+        bias_t = psum_head.tile([P, P], BF16, tag="transposed")
+        nc.tensor.transpose(bias_t[:], bias_rows[:], identity_bf16[:])
+        biases = keep.tile([P, FEATURE_TILES + 1], F32)
+        nc.vector.tensor_copy(out=biases[:], in_=bias_t[:, 0 : FEATURE_TILES + 1])
+        b1 = biases[:, FEATURE_TILES : FEATURE_TILES + 1]
+        b1_scaled = keep.tile([P, 1], F32)
+        nc.vector.tensor_scalar_mul(out=b1_scaled[:], in0=b1, scalar1=ALPHA)
 
         w0_grouped = keep.tile([P, HALVES, HIDDEN, PACK], BF16, align_bytes=64)
         w0_codes = keep.tile([P, HALVES, HIDDEN], U32, align_bytes=64)
@@ -136,7 +140,7 @@ def tile_graph_gan_pa_t_kernel(tc, x, fe_w0, fe_b0, fe_w1, fe_b1, out):
                         stop=True,
                     )
                 nc.scalar.activation(
-                    out=u_b0[:, ft, :], in_=uv[:, 0, :], func=IDENTITY, bias=b0[:, ft : ft + 1], scale=1.0
+                    out=u_b0[:, ft, :], in_=uv[:, 0, :], func=IDENTITY, bias=biases[:, ft : ft + 1], scale=1.0
                 )
                 nc.vector.tensor_copy(out=v[:, ft, :], in_=uv[:, 1, :])
 
@@ -150,11 +154,10 @@ def tile_graph_gan_pa_t_kernel(tc, x, fe_w0, fe_b0, fe_w1, fe_b1, out):
             scales=w1_scales[:].rearrange("p c n -> p (c n)"),
             in_=w1_grouped[:].rearrange("p c n t -> p (c n t)"),
         )
-        b1 = keep.tile([P, D_OUT], F32)
-        nc.vector.tensor_copy(out=b1[:], in_=b1_bf16[:])
 
-        def hidden_layer(block):
-            j_rows = slice((block // BLOCKS_PER_GRAPH) * NODES, (block // BLOCKS_PER_GRAPH + 1) * NODES)
+        def pair_sums(block):
+            graph = block // BLOCKS_PER_GRAPH
+            j_rows = slice(graph * NODES, (graph + 1) * NODES)
             z = sums.tile([P, PASSES, PACK, PAIRS], F32)
             for c in range(PASSES):
                 for t in range(PACK):
@@ -168,66 +171,76 @@ def tile_graph_gan_pa_t_kernel(tc, x, fe_w0, fe_b0, fe_w1, fe_b1, out):
                             bias=u_b0[:, ft, i_row : i_row + 1],
                             scale=1.0,
                         )
+            return z
+
+        def first_leaky_relu(z):
             e1 = hidden.tile([P, PASSES, PAIRS, PACK], BF16, align_bytes=64)
-            e1_planes = hidden.tile([P, PASSES, PACK, PAIRS_VIA_SCALAR], BF16)
             for c in range(PASSES):
-                z_words = z[:, c, :, 0:PAIRS_DIRECT].rearrange("p t w -> p w t")
+                z_words = z[:, c, :, :].rearrange("p t w -> p w t")
                 nc.vector.scalar_tensor_tensor(
-                    out=e1[:, c, 0:PAIRS_DIRECT, :], in0=z_words, scalar=ALPHA, in1=z_words, op0=MULT, op1=MAX
+                    out=e1[:, c, :, :], in0=z_words, scalar=ALPHA, in1=z_words, op0=MULT, op1=MAX
                 )
-                z_planes = z[:, c, :, PAIRS_DIRECT:PAIRS]
-                nc.vector.scalar_tensor_tensor(
-                    out=e1_planes[:, c, :, :], in0=z_planes, scalar=ALPHA, in1=z_planes, op0=MULT, op1=MAX
-                )
-                side_by_side(nc.scalar.copy, e1[:, c, PAIRS_DIRECT:PAIRS, :], e1_planes[:, c, :, :])
+            return e1
+
+        def quantise(e1):
             codes = hidden.tile([P, PASSES, PAIRS], U32, align_bytes=64)
             scales = hidden.tile([P, PASSES, PAIRS], U8, align_bytes=64)
-            for c in range(PASSES):
-                nc.vector.quantize_mx(
-                    out=codes[:, c, :].bitcast(FP8X4),
-                    scales=scales[:, c, :],
-                    in_=e1[:, c, :, :].rearrange("p w t -> p (w t)"),
-                )
+            nc.vector.quantize_mx(
+                out=codes[:].rearrange("p c w -> p (c w)").bitcast(FP8X4),
+                scales=scales[:].rearrange("p c w -> p (c w)"),
+                in_=e1[:].rearrange("p c w t -> p (c w t)"),
+            )
             return codes, scales
 
         def second_product(codes, scales):
-            y = psum_out.tile([P, PAIR_TILES, D_OUT], F32)
-            for g in range(PAIR_TILES):
-                pair_cols = slice(g * P, (g + 1) * P)
-                for c in range(PASSES):
-                    nc.tensor.matmul_mx(
-                        out=y[:, g, :],
-                        lhsT=codes[:, c, pair_cols].bitcast(FP8X4),
-                        lhsT_scale=scales[:, c, pair_cols],
-                        rhs=w1_codes[:, c, :].bitcast(FP8X4),
-                        rhs_scale=w1_scales[:, c, :],
-                        start=(c == 0),
-                        stop=(c == PASSES - 1),
-                    )
-            return y
+            y_t = psum_out.tile([P, PAIRS], F32)
+            for c in range(PASSES):
+                nc.tensor.matmul_mx(
+                    out=y_t[:],
+                    lhsT=w1_codes[:, c, :].bitcast(FP8X4),
+                    lhsT_scale=w1_scales[:, c, :],
+                    rhs=codes[:, c, :].bitcast(FP8X4),
+                    rhs_scale=scales[:, c, :],
+                    start=(c == 0),
+                    stop=(c == PASSES - 1),
+                )
+            return y_t
 
-        def finish(block, y):
-            biased = results.tile([P, PAIR_TILES, D_OUT], F32)
-            nc.vector.tensor_tensor(
-                out=biased[:],
-                in0=y[:],
-                in1=b1[:].unsqueeze(1).to_broadcast([P, PAIR_TILES, D_OUT]),
-                op=ADD,
-            )
-            result = results.tile([P, PAIR_TILES, D_OUT], F32)
+        def second_leaky_relu(y_t):
+            scaled = results.tile([P, PAIRS], F32)
+            nc.scalar.activation(out=scaled[:], in_=y_t[:], func=IDENTITY, bias=b1_scaled[:], scale=ALPHA)
+            out_t = results.tile([P, PAIRS], F32)
             nc.vector.scalar_tensor_tensor(
-                out=result[:], in0=biased[:], scalar=ALPHA, in1=biased[:], op0=MULT, op1=MAX
+                out=out_t[:], in0=y_t[:], scalar=b1, in1=scaled[:], op0=ADD, op1=MAX
             )
+            return out_t
+
+        def turn_and_store(block, out_t):
+            turned = psum_out.tile([P, PAIR_TILES, D_OUT], F32)
+            for g in range(PAIR_TILES):
+                nc.tensor.transpose(turned[:, g, :], out_t[:, g * P : (g + 1) * P], identity_f32[:])
+            result = results.tile([P, PAIR_TILES, D_OUT], F32)
+            nc.scalar.copy(out=result[:], in_=turned[:])
             nc.sync.dma_start(
                 out=out_rows[block * PAIRS : (block + 1) * PAIRS, :].rearrange("(g p) n -> p g n", p=P),
                 in_=result[:],
             )
 
-        waiting = None
-        for block in range(BLOCKS):
-            codes, scales = hidden_layer(block)
-            y = second_product(codes, scales)
-            if waiting is not None:
-                finish(block - 1, waiting)
-            waiting = y
-        finish(BLOCKS - 1, waiting)
+        sums_of = {}
+        product_of = {}
+        output_of = {}
+        for block in range(SUMS_AHEAD):
+            sums_of[block] = pair_sums(block)
+        for block in range(BLOCKS + 2):
+            if block < BLOCKS:
+                e1 = first_leaky_relu(sums_of[block])
+            if 1 <= block <= BLOCKS:
+                output_of[block - 1] = second_leaky_relu(product_of[block - 1])
+            if block < BLOCKS:
+                codes, scales = quantise(e1)
+            if block >= 2:
+                turn_and_store(block - 2, output_of[block - 2])
+            if block < BLOCKS:
+                product_of[block] = second_product(codes, scales)
+            if block + SUMS_AHEAD < BLOCKS:
+                sums_of[block + SUMS_AHEAD] = pair_sums(block + SUMS_AHEAD)

from contextlib import ExitStack

import concourse.mybir as mybir
from concourse.masks import make_identity

BF16 = mybir.dt.bfloat16
F32 = mybir.dt.float32
U32 = mybir.dt.uint32
U8 = mybir.dt.uint8
FP8X4 = mybir.dt.float8_e4m3fn_x4
ADD = mybir.AluOpType.add
MULT = mybir.AluOpType.mult
MAX = mybir.AluOpType.max
IDENTITY = mybir.ActivationFunctionType.Identity

P = 128
PACK = 4
K_PASS = P * PACK

GRAPHS, NODES, D_IN, HIDDEN, D_OUT = 4, 64, 512, 1024, 128
ROWS = GRAPHS * NODES
ROW_TILES = ROWS // P
HALVES = 2
PASSES = HIDDEN // K_PASS
FEATURE_TILES = HIDDEN // P
ALPHA = 0.2

I_PER_BLOCK = 8
PAIRS = I_PER_BLOCK * NODES
PAIR_TILES = PAIRS // P
BLOCKS = ROWS // I_PER_BLOCK
BLOCKS_PER_GRAPH = NODES // I_PER_BLOCK
SUMS_AHEAD = 2

FLOPS = 2 * HALVES * ROWS * D_IN * HIDDEN + 2 * ROWS * NODES * HIDDEN * D_OUT


def side_by_side(copy, grouped, planes):
    copy(
        out=grouped.rearrange("p (g i) t -> p g t i", i=4),
        in_=planes.rearrange("p t (g i) -> p g t i", i=4),
    )


def tile_graph_gan_pa_t_kernel(tc, x, fe_w0, fe_b0, fe_w1, fe_b1, out):
    nc = tc.nc
    x_rows = x.flatten_outer_dims()
    out_rows = out.flatten_outer_dims()

    with ExitStack() as stack:
        keep = stack.enter_context(tc.tile_pool(name="keep", bufs=1))
        sums = stack.enter_context(tc.tile_pool(name="sums", bufs=SUMS_AHEAD + 1))
        hidden = stack.enter_context(tc.tile_pool(name="hidden", bufs=3))
        results = stack.enter_context(tc.tile_pool(name="results", bufs=3))
        psum_head = stack.enter_context(tc.psum_pool(name="psum_head", bufs=2))
        psum_out = stack.enter_context(tc.psum_pool(name="psum_out", bufs=2))

        identity_bf16 = keep.tile([P, P], BF16)
        make_identity(nc, identity_bf16[:])
        identity_f32 = keep.tile([P, P], F32)
        make_identity(nc, identity_f32[:])
        bias_rows = keep.tile([P, P], BF16)
        nc.gpsimd.memset(bias_rows[:], 0.0)

        x_sb = keep.tile([P, ROW_TILES, D_IN], BF16)
        nc.sync.dma_start(out=x_sb[:], in_=x_rows.rearrange("(r p) d -> p r d", p=P))
        nc.scalar.dma_start(
            out=bias_rows[0:FEATURE_TILES, :], in_=fe_b0.rearrange("(r p) -> r p", p=P)
        )
        nc.scalar.dma_start(
            out=bias_rows[FEATURE_TILES : FEATURE_TILES + 1, :], in_=fe_b1.rearrange("(r p) -> r p", p=P)
        )
        w0_planes = keep.tile([P, HALVES, PACK, HIDDEN], BF16)
        for c in range(PASSES):
            f_cols = slice(c * K_PASS, (c + 1) * K_PASS)
            for h in range(HALVES):
                nc.sync.dma_start(
                    out=w0_planes[:, h, :, f_cols],
                    in_=fe_w0[h * D_IN : (h + 1) * D_IN, f_cols].rearrange(
                        "(t p) f -> p t f", p=P
                    ),
                )
        w1_planes = keep.tile([P, PASSES, PACK, D_OUT], BF16)
        nc.sync.dma_start(
            out=w1_planes[:], in_=fe_w1.rearrange("(c t p) n -> p c t n", t=PACK, p=P)
        )

        x_grouped = keep.tile([P, ROWS, PACK], BF16, align_bytes=64)
        for r in range(ROW_TILES):
            x_t = psum_head.tile([P, PACK, P], BF16, tag="transposed")
            for t in range(PACK):
                nc.tensor.transpose(x_t[:, t, :], x_sb[:, r, t * P : (t + 1) * P], identity_bf16[:])
            nc.vector.tensor_copy(
                out=x_grouped[:, r * P : (r + 1) * P, :], in_=x_t[:].rearrange("p t r -> p r t")
            )
        x_codes = keep.tile([P, ROWS], U32, align_bytes=64)
        x_scales = keep.tile([P, ROWS], U8, align_bytes=64)
        nc.vector.quantize_mx(
            out=x_codes[:].bitcast(FP8X4),
            scales=x_scales[:],
            in_=x_grouped[:].rearrange("p r t -> p (r t)"),
        )

        bias_t = psum_head.tile([P, P], BF16, tag="transposed")
        nc.tensor.transpose(bias_t[:], bias_rows[:], identity_bf16[:])
        biases = keep.tile([P, FEATURE_TILES + 1], F32)
        nc.vector.tensor_copy(out=biases[:], in_=bias_t[:, 0 : FEATURE_TILES + 1])
        b1 = biases[:, FEATURE_TILES : FEATURE_TILES + 1]
        b1_scaled = keep.tile([P, 1], F32)
        nc.vector.tensor_scalar_mul(out=b1_scaled[:], in0=b1, scalar1=ALPHA)

        w0_grouped = keep.tile([P, HALVES, HIDDEN, PACK], BF16, align_bytes=64)
        w0_codes = keep.tile([P, HALVES, HIDDEN], U32, align_bytes=64)
        w0_scales = keep.tile([P, HALVES, HIDDEN], U8, align_bytes=64)
        u_b0 = keep.tile([P, FEATURE_TILES, ROWS], F32)
        v = keep.tile([P, FEATURE_TILES, ROWS], F32)
        for c in range(PASSES):
            f_cols = slice(c * K_PASS, (c + 1) * K_PASS)
            for h in range(HALVES):
                side_by_side(
                    nc.vector.tensor_copy, w0_grouped[:, h, f_cols, :], w0_planes[:, h, :, f_cols]
                )
            for h in range(HALVES):
                nc.vector.quantize_mx(
                    out=w0_codes[:, h, f_cols].bitcast(FP8X4),
                    scales=w0_scales[:, h, f_cols],
                    in_=w0_grouped[:, h, f_cols, :].rearrange("p f t -> p (f t)"),
                )
            for ft in range(c * PACK, (c + 1) * PACK):
                tile_cols = slice(ft * P, (ft + 1) * P)
                uv = psum_head.tile([P, HALVES, ROWS], F32)
                for h in range(HALVES):
                    nc.tensor.matmul_mx(
                        out=uv[:, h, :],
                        lhsT=w0_codes[:, h, tile_cols].bitcast(FP8X4),
                        lhsT_scale=w0_scales[:, h, tile_cols],
                        rhs=x_codes[:].bitcast(FP8X4),
                        rhs_scale=x_scales[:],
                        start=True,
                        stop=True,
                    )
                nc.scalar.activation(
                    out=u_b0[:, ft, :], in_=uv[:, 0, :], func=IDENTITY, bias=biases[:, ft : ft + 1], scale=1.0
                )
                nc.vector.tensor_copy(out=v[:, ft, :], in_=uv[:, 1, :])

        w1_grouped = keep.tile([P, PASSES, D_OUT, PACK], BF16, align_bytes=64)
        for c in range(PASSES):
            side_by_side(nc.scalar.copy, w1_grouped[:, c, :, :], w1_planes[:, c, :, :])
        w1_codes = keep.tile([P, PASSES, D_OUT], U32, align_bytes=64)
        w1_scales = keep.tile([P, PASSES, D_OUT], U8, align_bytes=64)
        nc.vector.quantize_mx(
            out=w1_codes[:].rearrange("p c n -> p (c n)").bitcast(FP8X4),
            scales=w1_scales[:].rearrange("p c n -> p (c n)"),
            in_=w1_grouped[:].rearrange("p c n t -> p (c n t)"),
        )

        def pair_sums(block):
            graph = block // BLOCKS_PER_GRAPH
            j_rows = slice(graph * NODES, (graph + 1) * NODES)
            z = sums.tile([P, PASSES, PACK, PAIRS], F32)
            for c in range(PASSES):
                for t in range(PACK):
                    ft = c * PACK + t
                    for i in range(I_PER_BLOCK):
                        i_row = block * I_PER_BLOCK + i
                        nc.scalar.activation(
                            out=z[:, c, t, i * NODES : (i + 1) * NODES],
                            in_=v[:, ft, j_rows],
                            func=IDENTITY,
                            bias=u_b0[:, ft, i_row : i_row + 1],
                            scale=1.0,
                        )
            return z

        def first_leaky_relu(z):
            e1 = hidden.tile([P, PASSES, PAIRS, PACK], BF16, align_bytes=64)
            for c in range(PASSES):
                z_words = z[:, c, :, :].rearrange("p t w -> p w t")
                nc.vector.scalar_tensor_tensor(
                    out=e1[:, c, :, :], in0=z_words, scalar=ALPHA, in1=z_words, op0=MULT, op1=MAX
                )
            return e1

        def quantise(e1):
            codes = hidden.tile([P, PASSES, PAIRS], U32, align_bytes=64)
            scales = hidden.tile([P, PASSES, PAIRS], U8, align_bytes=64)
            nc.vector.quantize_mx(
                out=codes[:].rearrange("p c w -> p (c w)").bitcast(FP8X4),
                scales=scales[:].rearrange("p c w -> p (c w)"),
                in_=e1[:].rearrange("p c w t -> p (c w t)"),
            )
            return codes, scales

        def second_product(codes, scales):
            y_t = psum_out.tile([P, PAIRS], F32)
            for c in range(PASSES):
                nc.tensor.matmul_mx(
                    out=y_t[:],
                    lhsT=w1_codes[:, c, :].bitcast(FP8X4),
                    lhsT_scale=w1_scales[:, c, :],
                    rhs=codes[:, c, :].bitcast(FP8X4),
                    rhs_scale=scales[:, c, :],
                    start=(c == 0),
                    stop=(c == PASSES - 1),
                )
            return y_t

        def second_leaky_relu(y_t):
            scaled = results.tile([P, PAIRS], F32)
            nc.scalar.activation(out=scaled[:], in_=y_t[:], func=IDENTITY, bias=b1_scaled[:], scale=ALPHA)
            out_t = results.tile([P, PAIRS], F32)
            nc.vector.scalar_tensor_tensor(
                out=out_t[:], in0=y_t[:], scalar=b1, in1=scaled[:], op0=ADD, op1=MAX
            )
            return out_t

        def turn_and_store(block, out_t):
            turned = psum_out.tile([P, PAIR_TILES, D_OUT], F32)
            for g in range(PAIR_TILES):
                nc.tensor.transpose(turned[:, g, :], out_t[:, g * P : (g + 1) * P], identity_f32[:])
            result = results.tile([P, PAIR_TILES, D_OUT], F32)
            nc.scalar.copy(out=result[:], in_=turned[:])
            nc.sync.dma_start(
                out=out_rows[block * PAIRS : (block + 1) * PAIRS, :].rearrange("(g p) n -> p g n", p=P),
                in_=result[:],
            )

        sums_of = {}
        product_of = {}
        output_of = {}
        for block in range(SUMS_AHEAD):
            sums_of[block] = pair_sums(block)
        for block in range(BLOCKS + 2):
            if block < BLOCKS:
                e1 = first_leaky_relu(sums_of[block])
            if 1 <= block <= BLOCKS:
                output_of[block - 1] = second_leaky_relu(product_of[block - 1])
            if block < BLOCKS:
                codes, scales = quantise(e1)
            if block >= 2:
                turn_and_store(block - 2, output_of[block - 2])
            if block < BLOCKS:
                product_of[block] = second_product(codes, scales)
            if block + SUMS_AHEAD < BLOCKS:
                sums_of[block + SUMS_AHEAD] = pair_sums(block + SUMS_AHEAD)
